import numpy as np
import ml_dtypes


def mxq(x, axis, fmt="e4m3"):
    dtype, down = {"e4m3": (ml_dtypes.float8_e4m3fn, 7), "e5m2": (ml_dtypes.float8_e5m2, 14)}[fmt]
    v = np.moveaxis(np.asarray(x, np.float32).astype(ml_dtypes.bfloat16).astype(np.float64), axis, -1)
    blocks = v.reshape(v.shape[:-1] + (-1, 32))
    amax = np.abs(blocks).max(-1, keepdims=True)
    byte = np.maximum(np.where(amax > 0, np.frexp(amax)[1] - 1 + 127, 0) - down, 1)
    scale = np.exp2(byte - 127.0)
    codes = (blocks / scale).astype(np.float32).astype(dtype).astype(np.float64)
    return np.moveaxis((codes * scale).reshape(v.shape), -1, axis)


WIDE = False


def mx_kscale(k):
    if not WIDE:
        return np.ones(k)
    levels = np.array([10, -10, 5, -5, 0])
    a = np.random.permutation(np.resize(levels, k // 512 * 4)).reshape(k // 512, 4)
    idx = np.arange(k)
    return np.exp2(a[idx // 512, idx % 128 // 32])


BF16 = ml_dtypes.bfloat16


def bf(x):
    return np.asarray(x, np.float32).astype(BF16)


def f64(x):
    return np.asarray(x).astype(np.float64)


E2M1 = np.array([0.0, 0.5, 1.0, 1.5, 2.0, 3.0, 4.0, 6.0, -0.0, -0.5, -1.0, -1.5, -2.0, -3.0, -4.0, -6.0])


def pack_weight(w, fmt):
    k, n = w.shape
    w = f64(bf(w)).reshape(k // 32, 32, n)
    amax = np.abs(w).max(1)
    if fmt == "e4m3":
        byte = np.frexp(amax)[1] - 1 + 127 - 7
    else:
        mant, ex = np.frexp(amax / 6.0)
        byte = np.where(mant > 0.5, ex, ex - 1) + 127
    byte = np.clip(np.where(amax > 0, byte, 1), 1, 254)
    scaled = (w * np.exp2(127.0 - byte)[:, None, :]).reshape(k, n).astype(np.float32)
    by_word = np.ascontiguousarray(scaled.reshape(k // 512, 128, 4, n).transpose(0, 1, 3, 2))
    if fmt == "e4m3":
        words = by_word.astype(ml_dtypes.float8_e4m3fn).view(np.uint8)
    else:
        c = by_word.astype(ml_dtypes.float4_e2m1fn).view(np.uint8) & 0xF
        words = c[..., 0::2] | (c[..., 1::2] << 4)
    return np.ascontiguousarray(words), np.ascontiguousarray(byte.astype(np.uint8).reshape(k // 512, 16, n))


def unpack_weight(words, scales, fmt):
    g, p, n, _ = words.shape
    if fmt == "e4m3":
        vals = np.ascontiguousarray(words).view(ml_dtypes.float8_e4m3fn).astype(np.float64)
    else:
        nib = np.empty((g, p, n, 4), np.uint8)
        nib[..., 0::2] = words & 0xF
        nib[..., 1::2] = words >> 4
        vals = E2M1[nib]
    vals = vals * np.repeat(np.exp2(scales.astype(np.float64) - 127.0), 8, axis=1)[..., None]
    return vals.transpose(0, 1, 3, 2).reshape(g * 512, n)


C, H, W, CO, G = 1024, 32, 16, 4096, 128
K = 4 * C
P = (H // 2) * (W // 2)
EPS = 1e-5
FMT = "e4m3"


def haar_bands(x):
    xr = x.reshape(C, H // 2, 2, W // 2, 2)
    x00 = xr[:, :, 0, :, 0]
    x01 = xr[:, :, 0, :, 1]
    x10 = xr[:, :, 1, :, 0]
    x11 = xr[:, :, 1, :, 1]
    half = 0.5
    LL = (x00 + x01 + x10 + x11) * half
    HL = (-x00 - x01 + x10 + x11) * half
    LH = (-x00 + x01 - x10 + x11) * half
    HH = (x00 - x01 - x10 + x11) * half
    return LL, HL, LH, HH


def group_norm(y, scale, bias, groups):
    c, h, w = y.shape
    yg = y.reshape(groups, c // groups, h, w)
    mean = np.mean(yg, axis=(1, 2, 3), keepdims=True)
    var = np.mean(np.square(yg - mean), axis=(1, 2, 3), keepdims=True)
    yn = ((yg - mean) / np.sqrt(var + EPS)).reshape(c, h, w)
    return yn * scale[:, None, None] + bias[:, None, None]


def setup_inputs():
    s = mx_kscale(K)
    x = bf(np.random.standard_normal((C, H, W)))
    gn_scale = bf((1.0 + 0.1 * np.random.standard_normal(K)) * s)
    gn_bias = bf(0.1 * np.random.standard_normal(K) * s)
    w_proj = np.random.standard_normal((CO, K)) / np.sqrt(K) / s[None, :]
    words, scales = pack_weight(np.ascontiguousarray(w_proj.T), FMT)
    return {"x": x,
            "gn_scale": gn_scale,
            "gn_bias": gn_bias,
            "w_proj_words": words,
            "w_proj_scales": scales}


def reference(x, gn_scale, gn_bias, w_proj_words, w_proj_scales):
    LL, HL, LH, HH = haar_bands(f64(x))
    y = np.concatenate([LL, HL, LH, HH], axis=0)
    y = group_norm(y, f64(gn_scale), f64(gn_bias), G)
    z = unpack_weight(w_proj_words, w_proj_scales, FMT).T @ mxq(y.reshape(K, P), 0, "e4m3")
    return np.maximum(z, 0.0).reshape(CO, H // 2, W // 2)

@@ -1,0 +1,278 @@
+from contextlib import ExitStack
+
+import concourse.mybir as mybir
+from concourse.masks import make_identity
+
+F32 = mybir.dt.float32
+BF16 = mybir.dt.bfloat16
+I32 = mybir.dt.int32
+U32 = mybir.dt.uint32
+U8 = mybir.dt.uint8
+FP8X4 = mybir.dt.float8_e4m3fn_x4
+ALU = mybir.AluOpType
+ACT = mybir.ActivationFunctionType
+AX = mybir.AxisListType
+
+P = 128
+C = 1024
+CO = 4096
+K = 4 * C
+PIX = 128
+PASSES = K // 512
+BANK = 512
+EPS4 = 4.0 * 1e-5
+FLOPS = 2 * CO * K * PIX
+
+PIECES = [(g, 0, 8) for g in range(6)] + [(6, 0, 4), (7, 0, 4), (6, 4, 8), (7, 4, 8)]
+VECTOR_OF_8 = 5
+
+
+def tile_hwdconv_w_kernel(tc, x, gn_scale, gn_bias, w_proj_words, w_proj_scales, out):
+    nc = tc.nc
+    with ExitStack() as ctx:
+        keep = ctx.enter_context(tc.tile_pool(name="keep", bufs=1))
+        psum = ctx.enter_context(tc.psum_pool(name="psum", bufs=1))
+        ctx.enter_context(tc.manual_schedule())
+
+        eps_t = keep.tile([P, 1], F32, name="eps_t")
+        warm = keep.tile([P, 1], F32, name="warm")
+        gtile = keep.tile([P, 512], BF16, name="gtile")
+        planes = keep.tile([P, 2, CO], U8, name="planes", align_bytes=64)
+        ident = keep.tile([P, P], F32, name="ident")
+        blk = keep.tile([P, 16], F32, name="blk")
+        bd = keep.tile([P, P], F32, name="bd")
+        xt = keep.tile([P, 2, 2048], BF16, name="xt")
+        prm = keep.tile([P, 16, 4], F32, name="prm")
+
+        nc.vector.memset(eps_t[:], EPS4)
+        nc.vector.memset(gtile[:].bitcast(I32), 0)
+        nc.vector.memset(planes[:].bitcast(I32), 0)
+        make_identity(nc, ident[:])
+
+        xv = x.rearrange("(h p t) r c -> h p (t r c)", h=2, p=P, t=4)
+        for h in range(2):
+            nc.sync.dma_start(out=xt[:, h, :], in_=xv[h])
+        nc.scalar.dma_start(out=gtile[0:8, :], in_=gn_scale.rearrange("(g k) -> g k", g=8))
+        nc.scalar.dma_start(out=gtile[8:16, :], in_=gn_bias.rearrange("(g k) -> g k", g=8))
+        nc.scalar.activation(out=warm[:], in_=eps_t[:], func=ACT.Sqrt)
+
+        for hh in range(2):
+            for q in (0, 2, 1, 3):
+                nc.sync.dma_start(
+                    out=planes[32 * q : 32 * q + 16, hh, :].bitcast(I32),
+                    in_=w_proj_scales[4 * hh : 4 * hh + 4, 4 * q : 4 * q + 4, :].bitcast(I32),
+                )
+
+        w_tiles = []
+        for g, c0, c1 in PIECES:
+            wt = keep.tile([P, (c1 - c0) * BANK], U32, name="w%d_%d" % (g, c0), align_bytes=64)
+            nc.sync.dma_start(
+                out=wt[:].bitcast(I32),
+                in_=w_proj_words[g].rearrange("p n t -> p (n t)")[:, 4 * BANK * c0 : 4 * BANK * c1].bitcast(I32),
+            )
+            w_tiles.append(wt)
+
+        nc.vector.tensor_reduce(out=blk[:], in_=ident[:].rearrange("p (a e) -> p a e", e=8), axis=AX.X, op=ALU.add)
+        nc.vector.tensor_scalar(
+            out=bd[:].rearrange("p (a e) -> p a e", e=8),
+            in0=blk[:].unsqueeze(2).to_broadcast([P, 16, 8]),
+            scalar1=1.0 / 4096.0,
+            scalar2=None,
+            op0=ALU.mult,
+        )
+
+        pt = psum.tile([P, 2, P], F32, name="pt", tag="b0")
+        gw = gtile[:].bitcast(F32)
+        for u in range(2):
+            nc.tensor.transpose(out=pt[:, u, :], in_=gw[:, u:256:2], identity=ident[:])
+        nc.scalar.copy(
+            out=prm[:].rearrange("p r (u e) -> p r u e", e=2),
+            in_=pt[:, :, 0:16].bitcast(BF16).rearrange("p u (r e) -> p r u e", e=2),
+        )
+
+        yw = keep.tile([P, PASSES * PIX], U32, name="yw", align_bytes=64)
+        ys = keep.tile([P, PASSES * PIX], U8, name="ys", align_bytes=64)
+        junk = keep.tile([P, 512], BF16, name="junk")
+
+        st = {}
+        for hf in range(2):
+            st["sd", hf] = keep.tile([P, 2, 1024], F32, name="sd%d" % hf, tag="sd%d" % hf)
+            st["bnd", hf] = keep.tile([P, 4, 512], F32, name="bnd%d" % hf, tag="bnd%d" % hf)
+            for nm in ("sums", "negm", "ssq", "std", "rstd"):
+                st[nm, hf] = keep.tile([P, 4], F32, name="%s%d" % (nm, hf))
+            for nm in ("a", "tmp", "b"):
+                st[nm, hf] = keep.tile([P, 4, 4], F32, name="%s%d" % (nm, hf))
+            st["yb", hf] = keep.tile([P, 2048], BF16, name="yb%d" % hf)
+            st["grp", hf] = keep.tile([P, 2048], BF16, name="grp%d" % hf, align_bytes=64)
+
+        def haar(hf):
+            sd = st["sd", hf]
+            for h in range(2):
+                pair = xt[:, h, :].rearrange("p (m b) -> p m b", b=2)
+                if hf == 0:
+                    nc.vector.tensor_tensor(out=sd[:, h, :], in0=pair[:, :, 0], in1=pair[:, :, 1], op=ALU.add)
+                else:
+                    nc.vector.tensor_tensor(out=sd[:, h, :], in0=pair[:, :, 1], in1=pair[:, :, 0], op=ALU.subtract)
+            for bb in range(2):
+                for h in range(2):
+                    gl = 2 * bb + h
+                    rows = sd[:, h, :].rearrange("p (q a j) -> p q a j", a=2, j=8)
+                    nc.vector.scalar_tensor_tensor(
+                        out=st["bnd", hf][:, gl, :].rearrange("p (q j) -> p q j", j=8),
+                        in0=rows[:, :, 0, :],
+                        scalar=1.0 if bb == 0 else -1.0,
+                        in1=rows[:, :, 1, :],
+                        op0=ALU.mult,
+                        op1=ALU.add,
+                        accum_out=st["sums", hf][:, gl : gl + 1],
+                    )
+
+        def mean(hf, tag):
+            pm = psum.tile([P, 4], F32, name="pm%d" % hf, tag=tag)
+            nc.tensor.matmul(out=pm[:], lhsT=bd[:], rhs=st["sums", hf][:], start=True, stop=True)
+            return pm
+
+        def squares(hf, pm):
+            nc.scalar.mul(out=st["negm", hf][:], in_=pm[:], mul=-1.0)
+            for gl in range(4):
+                nc.scalar.activation(
+                    out=junk[:],
+                    in_=st["bnd", hf][:, gl, :],
+                    func=ACT.Square,
+                    bias=st["negm", hf][:, gl : gl + 1],
+                    scale=1.0,
+                    accum_out=st["ssq", hf][:, gl : gl + 1],
+                )
+
+        def deviation(hf, tag):
+            pv = psum.tile([P, 4], F32, name="pv%d" % hf, tag=tag)
+            nc.tensor.matmul(out=pv[:], lhsT=bd[:], rhs=st["ssq", hf][:], start=True, stop=True)
+            nc.scalar.activation(out=st["std", hf][:], in_=pv[:], func=ACT.Sqrt, bias=eps_t[:, 0:1], scale=1.0)
+
+        def coefficients(hf):
+            nc.vector.reciprocal(out=st["rstd", hf][:], in_=st["std", hf][:])
+            nc.vector.tensor_tensor(
+                out=st["a", hf][:],
+                in0=prm[:, 4 * hf : 4 * hf + 4, :],
+                in1=st["rstd", hf][:].unsqueeze(2).to_broadcast([P, 4, 4]),
+                op=ALU.mult,
+            )
+            nc.vector.tensor_tensor(
+                out=st["tmp", hf][:],
+                in0=st["a", hf][:],
+                in1=st["negm", hf][:].unsqueeze(2).to_broadcast([P, 4, 4]),
+                op=ALU.mult,
+            )
+            nc.vector.tensor_tensor(
+                out=st["b", hf][:], in0=st["tmp", hf][:], in1=prm[:, 8 + 4 * hf : 12 + 4 * hf, :], op=ALU.add
+            )
+
+        def affine(hf):
+            for gl in range(4):
+                for t in range(4):
+                    i = 4 * gl + t
+                    dst = st["yb", hf][:, PIX * i : PIX * (i + 1)]
+                    src = st["bnd", hf][:, gl, PIX * t : PIX * (t + 1)]
+                    gain = st["a", hf][:, gl, t : t + 1]
+                    bias = st["b", hf][:, gl, t : t + 1]
+                    if i % 8 < VECTOR_OF_8:
+                        nc.vector.tensor_scalar(
+                            out=dst, in0=src, scalar1=gain, scalar2=bias, op0=ALU.mult, op1=ALU.add
+                        )
+                    else:
+                        nc.scalar.activation(out=dst, in_=src, func=ACT.Identity, bias=bias, scale=gain)
+
+        def regroup(hf):
+            nc.vector.tensor_copy(
+                out=st["grp", hf][:].rearrange("p (g c i t) -> p g c t i", g=4, c=32, i=4, t=4),
+                in_=st["yb", hf][:].rearrange("p (g t c i) -> p g c t i", g=4, t=4, c=32, i=4),
+            )
+
+        def quantise(hf):
+            nc.vector.quantize_mx(
+                out=yw[:, 512 * hf : 512 * (hf + 1)].bitcast(FP8X4),
+                scales=ys[:, 512 * hf : 512 * (hf + 1)],
+                in_=st["grp", hf][:],
+            )
+
+        haar(0)
+        pm0 = mean(0, "b1")
+        squares(0, pm0)
+        deviation(0, "b2")
+        haar(1)
+        pm1 = mean(1, "b3")
+        coefficients(0)
+        affine(0)
+        squares(1, pm1)
+        deviation(1, "b4")
+        regroup(0)
+        quantise(0)
+        coefficients(1)
+        affine(1)
+        regroup(1)
+        quantise(1)
+
+        acc = {}
+        zs = {}
+        ot = {}
+        out_v = out.rearrange("(c p j) h w -> c p (j h w)", p=P, j=4)
+
+        def passes(i):
+            g, c0, c1 = PIECES[i]
+            for c in range(c0, c1):
+                if g == 0:
+                    acc[c] = psum.tile([P, BANK], F32, name="acc%d" % c, tag="b%d" % c)
+                k = 4 * (g % 4)
+                nc.tensor.matmul_mx(
+                    out=acc[c][:],
+                    lhsT=yw[:, PIX * g : PIX * (g + 1)].bitcast(FP8X4),
+                    lhsT_scale=ys[:, PIX * g : PIX * (g + 1)],
+                    rhs=w_tiles[i][:, BANK * (c - c0) : BANK * (c - c0 + 1)].bitcast(FP8X4),
+                    rhs_scale=planes[k:P, g // 4, BANK * c : BANK * (c + 1)],
+                    start=(g == 0),
+                    stop=(g == PASSES - 1),
+                )
+
+        def relu(c):
+            hf = c // 4
+            if c % 4 == 0:
+                zs[hf] = keep.tile([P, 4, 4, P], F32, name="zs%d" % hf, tag="bnd%d" % hf)
+            dst = zs[hf][:, c % 4, :, :]
+            src = acc[c][:].rearrange("q (p j) -> q j p", j=4)
+            if c % 2 == 0:
+                nc.vector.tensor_scalar_max(out=dst, in0=src, scalar1=0.0)
+            else:
+                nc.scalar.activation(out=dst, in_=src, func=ACT.Relu)
+
+        def flip(c):
+            zt = psum.tile([P, 4, P], F32, name="zt%d" % c, tag="b%d" % c)
+            for j in range(4):
+                nc.tensor.transpose(out=zt[:, j, :], in_=zs[c // 4][:, c % 4, j, :], identity=ident[:])
+            return zt
+
+        def leave(c, zt):
+            hf = c // 4
+            if c % 4 == 0:
+                ot[hf] = keep.tile([P, 4, BANK], F32, name="ot%d" % hf, tag="sd%d" % hf)
+            dst = ot[hf][:, c % 4, :]
+            src = zt[:].rearrange("p j q -> p (j q)")
+            if c % 2 == 0:
+                nc.vector.tensor_copy(out=dst, in_=src)
+            else:
+                nc.scalar.copy(out=dst, in_=src)
+            nc.sync.dma_start(out=out_v[c], in_=dst)
+
+        for i in range(8):
+            passes(i)
+        for c in range(4):
+            relu(c)
+        passes(8)
+        flipped = [flip(c) for c in range(4)]
+        for c in range(4):
+            leave(c, flipped[c])
+        passes(9)
+        for c in range(4, 8):
+            relu(c)
+        flipped = [flip(c) for c in range(4, 8)]
+        for c in range(4, 8):
+            leave(c, flipped[c - 4])

@@ -58,9 +58,9 @@ def tile_hwdconv_w_kernel(tc, x, gn_scale, gn_bias, w_proj_words, w_proj_scales,
 
         for hh in range(2):
             for q in (0, 2, 1, 3):
-                nc.sync.dma_start(
-                    out=planes[32 * q : 32 * q + 16, hh, :].bitcast(I32),
-                    in_=w_proj_scales[4 * hh : 4 * hh + 4, 4 * q : 4 * q + 4, :].bitcast(I32),
+                nc.gpsimd.dma_start(
+                    out=planes[32 * q : 32 * q + 16, hh, :].bitcast(F32),
+                    in_=w_proj_scales[4 * hh : 4 * hh + 4, 4 * q : 4 * q + 4, :].bitcast(F32),
                 )
 
         w_tiles = []

@@ -23,8 +23,13 @@ BANK = 512
 EPS4 = 4.0 * 1e-5
 FLOPS = 2 * CO * K * PIX
 
-PIECES = [(g, 0, 8) for g in range(6)] + [(6, 0, 4), (7, 0, 4), (6, 4, 8), (7, 4, 8)]
-VECTOR_OF_8 = 5
+PIECES = (
+    [(g, 0, 8) for g in range(4)]
+    + [(g, 0, 4) for g in range(4, 8)]
+    + [(g, 4, 8) for g in range(4, 7)]
+    + [(7, c, c + 1) for c in range(4, 8)]
+)
+VECTOR_SLICES = (16, 11)
 
 
 def tile_hwdconv_w_kernel(tc, x, gn_scale, gn_bias, w_proj_words, w_proj_scales, out):
@@ -58,9 +63,9 @@ def tile_hwdconv_w_kernel(tc, x, gn_scale, gn_bias, w_proj_words, w_proj_scales,
 
         for hh in range(2):
             for q in (0, 2, 1, 3):
-                nc.gpsimd.dma_start(
-                    out=planes[32 * q : 32 * q + 16, hh, :].bitcast(F32),
-                    in_=w_proj_scales[4 * hh : 4 * hh + 4, 4 * q : 4 * q + 4, :].bitcast(F32),
+                nc.sync.dma_start(
+                    out=planes[32 * q : 32 * q + 16, hh, :].bitcast(I32),
+                    in_=w_proj_scales[4 * hh : 4 * hh + 4, 4 * q : 4 * q + 4, :].bitcast(I32),
                 )
 
         w_tiles = []
@@ -175,7 +180,7 @@ def tile_hwdconv_w_kernel(tc, x, gn_scale, gn_bias, w_proj_words, w_proj_scales,
                     src = st["bnd", hf][:, gl, PIX * t : PIX * (t + 1)]
                     gain = st["a", hf][:, gl, t : t + 1]
                     bias = st["b", hf][:, gl, t : t + 1]
-                    if i % 8 < VECTOR_OF_8:
+                    if i < VECTOR_SLICES[hf]:
                         nc.vector.tensor_scalar(
                             out=dst, in0=src, scalar1=gain, scalar2=bias, op0=ALU.mult, op1=ALU.add
                         )
@@ -201,10 +206,10 @@ def tile_hwdconv_w_kernel(tc, x, gn_scale, gn_bias, w_proj_words, w_proj_scales,
         deviation(0, "b2")
         haar(1)
         pm1 = mean(1, "b3")
-        coefficients(0)
-        affine(0)
         squares(1, pm1)
         deviation(1, "b4")
+        coefficients(0)
+        affine(0)
         regroup(0)
         quantise(0)
         coefficients(1)
@@ -271,8 +276,14 @@ def tile_hwdconv_w_kernel(tc, x, gn_scale, gn_bias, w_proj_words, w_proj_scales,
         for c in range(4):
             leave(c, flipped[c])
         passes(9)
-        for c in range(4, 8):
+        passes(10)
+        for c in range(4, 7):
+            passes(7 + c)
             relu(c)
-        flipped = [flip(c) for c in range(4, 8)]
-        for c in range(4, 8):
-            leave(c, flipped[c - 4])
+        zt4 = flip(4)
+        leave(4, zt4)
+        passes(14)
+        relu(7)
+        for c in range(5, 8):
+            ztc = flip(c)
+            leave(c, ztc)

@@ -61,12 +61,15 @@ def tile_hwdconv_w_kernel(tc, x, gn_scale, gn_bias, w_proj_words, w_proj_scales,
         nc.scalar.dma_start(out=gtile[8:16, :], in_=gn_bias.rearrange("(g k) -> g k", g=8))
         nc.scalar.activation(out=warm[:], in_=eps_t[:], func=ACT.Sqrt)
 
-        for hh in range(2):
-            for q in (0, 2, 1, 3):
-                nc.sync.dma_start(
-                    out=planes[32 * q : 32 * q + 16, hh, :].bitcast(I32),
-                    in_=w_proj_scales[4 * hh : 4 * hh + 4, 4 * q : 4 * q + 4, :].bitcast(I32),
-                )
+        for q in (0, 2, 1, 3):
+            nc.sync.dma_start(
+                out=planes[32 * q : 32 * q + 16, 0, :].bitcast(I32),
+                in_=w_proj_scales[0:4, 4 * q : 4 * q + 4, :].bitcast(I32),
+            )
+            nc.gpsimd.dma_start(
+                out=planes[32 * q : 32 * q + 16, 1, :].bitcast(F32),
+                in_=w_proj_scales[4:8, 4 * q : 4 * q + 4, :].bitcast(F32),
+            )
 
         w_tiles = []
         for g, c0, c1 in PIECES:

from contextlib import ExitStack

import concourse.mybir as mybir
from concourse.masks import make_identity

F32 = mybir.dt.float32
BF16 = mybir.dt.bfloat16
I32 = mybir.dt.int32
U32 = mybir.dt.uint32
U8 = mybir.dt.uint8
FP8X4 = mybir.dt.float8_e4m3fn_x4
ALU = mybir.AluOpType
ACT = mybir.ActivationFunctionType
AX = mybir.AxisListType

P = 128
C = 1024
CO = 4096
K = 4 * C
PIX = 128
PASSES = K // 512
BANK = 512
EPS4 = 4.0 * 1e-5
FLOPS = 2 * CO * K * PIX

PIECES = (
    [(g, 0, 8) for g in range(4)]
    + [(g, 0, 4) for g in range(4, 8)]
    + [(g, 4, 8) for g in range(4, 7)]
    + [(7, c, c + 1) for c in range(4, 8)]
)
VECTOR_SLICES = (16, 11)


def tile_hwdconv_w_kernel(tc, x, gn_scale, gn_bias, w_proj_words, w_proj_scales, out):
    nc = tc.nc
    with ExitStack() as ctx:
        keep = ctx.enter_context(tc.tile_pool(name="keep", bufs=1))
        psum = ctx.enter_context(tc.psum_pool(name="psum", bufs=1))
        ctx.enter_context(tc.manual_schedule())

        eps_t = keep.tile([P, 1], F32, name="eps_t")
        warm = keep.tile([P, 1], F32, name="warm")
        gtile = keep.tile([P, 512], BF16, name="gtile")
        planes = keep.tile([P, 2, CO], U8, name="planes", align_bytes=64)
        ident = keep.tile([P, P], F32, name="ident")
        blk = keep.tile([P, 16], F32, name="blk")
        bd = keep.tile([P, P], F32, name="bd")
        xt = keep.tile([P, 2, 2048], BF16, name="xt")
        prm = keep.tile([P, 16, 4], F32, name="prm")

        nc.vector.memset(eps_t[:], EPS4)
        nc.vector.memset(gtile[:].bitcast(I32), 0)
        nc.vector.memset(planes[:].bitcast(I32), 0)
        make_identity(nc, ident[:])

        xv = x.rearrange("(h p t) r c -> h p (t r c)", h=2, p=P, t=4)
        for h in range(2):
            nc.sync.dma_start(out=xt[:, h, :], in_=xv[h])
        nc.scalar.dma_start(out=gtile[0:8, :], in_=gn_scale.rearrange("(g k) -> g k", g=8))
        nc.scalar.dma_start(out=gtile[8:16, :], in_=gn_bias.rearrange("(g k) -> g k", g=8))
        nc.scalar.activation(out=warm[:], in_=eps_t[:], func=ACT.Sqrt)

        for q in (0, 2, 1, 3):
            nc.sync.dma_start(
                out=planes[32 * q : 32 * q + 16, 0, :].bitcast(I32),
                in_=w_proj_scales[0:4, 4 * q : 4 * q + 4, :].bitcast(I32),
            )
            nc.gpsimd.dma_start(
                out=planes[32 * q : 32 * q + 16, 1, :].bitcast(F32),
                in_=w_proj_scales[4:8, 4 * q : 4 * q + 4, :].bitcast(F32),
            )

        w_tiles = []
        for g, c0, c1 in PIECES:
            wt = keep.tile([P, (c1 - c0) * BANK], U32, name="w%d_%d" % (g, c0), align_bytes=64)
            nc.sync.dma_start(
                out=wt[:].bitcast(I32),
                in_=w_proj_words[g].rearrange("p n t -> p (n t)")[:, 4 * BANK * c0 : 4 * BANK * c1].bitcast(I32),
            )
            w_tiles.append(wt)

        nc.vector.tensor_reduce(out=blk[:], in_=ident[:].rearrange("p (a e) -> p a e", e=8), axis=AX.X, op=ALU.add)
        nc.vector.tensor_scalar(
            out=bd[:].rearrange("p (a e) -> p a e", e=8),
            in0=blk[:].unsqueeze(2).to_broadcast([P, 16, 8]),
            scalar1=1.0 / 4096.0,
            scalar2=None,
            op0=ALU.mult,
        )

        pt = psum.tile([P, 2, P], F32, name="pt", tag="b0")
        gw = gtile[:].bitcast(F32)
        for u in range(2):
            nc.tensor.transpose(out=pt[:, u, :], in_=gw[:, u:256:2], identity=ident[:])
        nc.scalar.copy(
            out=prm[:].rearrange("p r (u e) -> p r u e", e=2),
            in_=pt[:, :, 0:16].bitcast(BF16).rearrange("p u (r e) -> p r u e", e=2),
        )

        yw = keep.tile([P, PASSES * PIX], U32, name="yw", align_bytes=64)
        ys = keep.tile([P, PASSES * PIX], U8, name="ys", align_bytes=64)
        junk = keep.tile([P, 512], BF16, name="junk")

        st = {}
        for hf in range(2):
            st["sd", hf] = keep.tile([P, 2, 1024], F32, name="sd%d" % hf, tag="sd%d" % hf)
            st["bnd", hf] = keep.tile([P, 4, 512], F32, name="bnd%d" % hf, tag="bnd%d" % hf)
            for nm in ("sums", "negm", "ssq", "std", "rstd"):
                st[nm, hf] = keep.tile([P, 4], F32, name="%s%d" % (nm, hf))
            for nm in ("a", "tmp", "b"):
                st[nm, hf] = keep.tile([P, 4, 4], F32, name="%s%d" % (nm, hf))
            st["yb", hf] = keep.tile([P, 2048], BF16, name="yb%d" % hf)
            st["grp", hf] = keep.tile([P, 2048], BF16, name="grp%d" % hf, align_bytes=64)

        def haar(hf):
            sd = st["sd", hf]
            for h in range(2):
                pair = xt[:, h, :].rearrange("p (m b) -> p m b", b=2)
                if hf == 0:
                    nc.vector.tensor_tensor(out=sd[:, h, :], in0=pair[:, :, 0], in1=pair[:, :, 1], op=ALU.add)
                else:
                    nc.vector.tensor_tensor(out=sd[:, h, :], in0=pair[:, :, 1], in1=pair[:, :, 0], op=ALU.subtract)
            for bb in range(2):
                for h in range(2):
                    gl = 2 * bb + h
                    rows = sd[:, h, :].rearrange("p (q a j) -> p q a j", a=2, j=8)
                    nc.vector.scalar_tensor_tensor(
                        out=st["bnd", hf][:, gl, :].rearrange("p (q j) -> p q j", j=8),
                        in0=rows[:, :, 0, :],
                        scalar=1.0 if bb == 0 else -1.0,
                        in1=rows[:, :, 1, :],
                        op0=ALU.mult,
                        op1=ALU.add,
                        accum_out=st["sums", hf][:, gl : gl + 1],
                    )

        def mean(hf, tag):
            pm = psum.tile([P, 4], F32, name="pm%d" % hf, tag=tag)
            nc.tensor.matmul(out=pm[:], lhsT=bd[:], rhs=st["sums", hf][:], start=True, stop=True)
            return pm

        def squares(hf, pm):
            nc.scalar.mul(out=st["negm", hf][:], in_=pm[:], mul=-1.0)
            for gl in range(4):
                nc.scalar.activation(
                    out=junk[:],
                    in_=st["bnd", hf][:, gl, :],
                    func=ACT.Square,
                    bias=st["negm", hf][:, gl : gl + 1],
                    scale=1.0,
                    accum_out=st["ssq", hf][:, gl : gl + 1],
                )

        def deviation(hf, tag):
            pv = psum.tile([P, 4], F32, name="pv%d" % hf, tag=tag)
            nc.tensor.matmul(out=pv[:], lhsT=bd[:], rhs=st["ssq", hf][:], start=True, stop=True)
            nc.scalar.activation(out=st["std", hf][:], in_=pv[:], func=ACT.Sqrt, bias=eps_t[:, 0:1], scale=1.0)

        def coefficients(hf):
            nc.vector.reciprocal(out=st["rstd", hf][:], in_=st["std", hf][:])
            nc.vector.tensor_tensor(
                out=st["a", hf][:],
                in0=prm[:, 4 * hf : 4 * hf + 4, :],
                in1=st["rstd", hf][:].unsqueeze(2).to_broadcast([P, 4, 4]),
                op=ALU.mult,
            )
            nc.vector.tensor_tensor(
                out=st["tmp", hf][:],
                in0=st["a", hf][:],
                in1=st["negm", hf][:].unsqueeze(2).to_broadcast([P, 4, 4]),
                op=ALU.mult,
            )
            nc.vector.tensor_tensor(
                out=st["b", hf][:], in0=st["tmp", hf][:], in1=prm[:, 8 + 4 * hf : 12 + 4 * hf, :], op=ALU.add
            )

        def affine(hf):
            for gl in range(4):
                for t in range(4):
                    i = 4 * gl + t
                    dst = st["yb", hf][:, PIX * i : PIX * (i + 1)]
                    src = st["bnd", hf][:, gl, PIX * t : PIX * (t + 1)]
                    gain = st["a", hf][:, gl, t : t + 1]
                    bias = st["b", hf][:, gl, t : t + 1]
                    if i < VECTOR_SLICES[hf]:
                        nc.vector.tensor_scalar(
                            out=dst, in0=src, scalar1=gain, scalar2=bias, op0=ALU.mult, op1=ALU.add
                        )
                    else:
                        nc.scalar.activation(out=dst, in_=src, func=ACT.Identity, bias=bias, scale=gain)

        def regroup(hf):
            nc.vector.tensor_copy(
                out=st["grp", hf][:].rearrange("p (g c i t) -> p g c t i", g=4, c=32, i=4, t=4),
                in_=st["yb", hf][:].rearrange("p (g t c i) -> p g c t i", g=4, t=4, c=32, i=4),
            )

        def quantise(hf):
            nc.vector.quantize_mx(
                out=yw[:, 512 * hf : 512 * (hf + 1)].bitcast(FP8X4),
                scales=ys[:, 512 * hf : 512 * (hf + 1)],
                in_=st["grp", hf][:],
            )

        haar(0)
        pm0 = mean(0, "b1")
        squares(0, pm0)
        deviation(0, "b2")
        haar(1)
        pm1 = mean(1, "b3")
        squares(1, pm1)
        deviation(1, "b4")
        coefficients(0)
        affine(0)
        regroup(0)
        quantise(0)
        coefficients(1)
        affine(1)
        regroup(1)
        quantise(1)

        acc = {}
        zs = {}
        ot = {}
        out_v = out.rearrange("(c p j) h w -> c p (j h w)", p=P, j=4)

        def passes(i):
            g, c0, c1 = PIECES[i]
            for c in range(c0, c1):
                if g == 0:
                    acc[c] = psum.tile([P, BANK], F32, name="acc%d" % c, tag="b%d" % c)
                k = 4 * (g % 4)
                nc.tensor.matmul_mx(
                    out=acc[c][:],
                    lhsT=yw[:, PIX * g : PIX * (g + 1)].bitcast(FP8X4),
                    lhsT_scale=ys[:, PIX * g : PIX * (g + 1)],
                    rhs=w_tiles[i][:, BANK * (c - c0) : BANK * (c - c0 + 1)].bitcast(FP8X4),
                    rhs_scale=planes[k:P, g // 4, BANK * c : BANK * (c + 1)],
                    start=(g == 0),
                    stop=(g == PASSES - 1),
                )

        def relu(c):
            hf = c // 4
            if c % 4 == 0:
                zs[hf] = keep.tile([P, 4, 4, P], F32, name="zs%d" % hf, tag="bnd%d" % hf)
            dst = zs[hf][:, c % 4, :, :]
            src = acc[c][:].rearrange("q (p j) -> q j p", j=4)
            if c % 2 == 0:
                nc.vector.tensor_scalar_max(out=dst, in0=src, scalar1=0.0)
            else:
                nc.scalar.activation(out=dst, in_=src, func=ACT.Relu)

        def flip(c):
            zt = psum.tile([P, 4, P], F32, name="zt%d" % c, tag="b%d" % c)
            for j in range(4):
                nc.tensor.transpose(out=zt[:, j, :], in_=zs[c // 4][:, c % 4, j, :], identity=ident[:])
            return zt

        def leave(c, zt):
            hf = c // 4
            if c % 4 == 0:
                ot[hf] = keep.tile([P, 4, BANK], F32, name="ot%d" % hf, tag="sd%d" % hf)
            dst = ot[hf][:, c % 4, :]
            src = zt[:].rearrange("p j q -> p (j q)")
            if c % 2 == 0:
                nc.vector.tensor_copy(out=dst, in_=src)
            else:
                nc.scalar.copy(out=dst, in_=src)
            nc.sync.dma_start(out=out_v[c], in_=dst)

        for i in range(8):
            passes(i)
        for c in range(4):
            relu(c)
        passes(8)
        flipped = [flip(c) for c in range(4)]
        for c in range(4):
            leave(c, flipped[c])
        passes(9)
        passes(10)
        for c in range(4, 7):
            passes(7 + c)
            relu(c)
        zt4 = flip(4)
        leave(4, zt4)
        passes(14)
        relu(7)
        for c in range(5, 8):
            ztc = flip(c)
            leave(c, ztc)
